import numpy as np
import ml_dtypes


def mxq(x, axis, fmt="e4m3"):
    dtype, down = {"e4m3": (ml_dtypes.float8_e4m3fn, 7), "e5m2": (ml_dtypes.float8_e5m2, 14)}[fmt]
    v = np.moveaxis(np.asarray(x, np.float32).astype(ml_dtypes.bfloat16).astype(np.float64), axis, -1)
    blocks = v.reshape(v.shape[:-1] + (-1, 32))
    amax = np.abs(blocks).max(-1, keepdims=True)
    byte = np.maximum(np.where(amax > 0, np.frexp(amax)[1] - 1 + 127, 0) - down, 1)
    scale = np.exp2(byte - 127.0)
    codes = (blocks / scale).astype(np.float32).astype(dtype).astype(np.float64)
    return np.moveaxis((codes * scale).reshape(v.shape), -1, axis)


WIDE = False


def mx_kscale(k):
    if not WIDE:
        return np.ones(k)
    levels = np.array([10, -10, 5, -5, 0])
    a = np.random.permutation(np.resize(levels, k // 512 * 4)).reshape(k // 512, 4)
    idx = np.arange(k)
    return np.exp2(a[idx // 512, idx % 128 // 32])


BF16 = ml_dtypes.bfloat16


def bf(x):
    return np.asarray(x, np.float32).astype(BF16)


def f64(x):
    return np.asarray(x).astype(np.float64)


E2M1 = np.array([0.0, 0.5, 1.0, 1.5, 2.0, 3.0, 4.0, 6.0, -0.0, -0.5, -1.0, -1.5, -2.0, -3.0, -4.0, -6.0])


def pack_weight(w, fmt):
    k, n = w.shape
    w = f64(bf(w)).reshape(k // 32, 32, n)
    amax = np.abs(w).max(1)
    if fmt == "e4m3":
        byte = np.frexp(amax)[1] - 1 + 127 - 7
    else:
        mant, ex = np.frexp(amax / 6.0)
        byte = np.where(mant > 0.5, ex, ex - 1) + 127
    byte = np.clip(np.where(amax > 0, byte, 1), 1, 254)
    scaled = (w * np.exp2(127.0 - byte)[:, None, :]).reshape(k, n).astype(np.float32)
    by_word = np.ascontiguousarray(scaled.reshape(k // 512, 128, 4, n).transpose(0, 1, 3, 2))
    if fmt == "e4m3":
        words = by_word.astype(ml_dtypes.float8_e4m3fn).view(np.uint8)
    else:
        c = by_word.astype(ml_dtypes.float4_e2m1fn).view(np.uint8) & 0xF
        words = c[..., 0::2] | (c[..., 1::2] << 4)
    return np.ascontiguousarray(words), np.ascontiguousarray(byte.astype(np.uint8).reshape(k // 512, 16, n))


def unpack_weight(words, scales, fmt):
    g, p, n, _ = words.shape
    if fmt == "e4m3":
        vals = np.ascontiguousarray(words).view(ml_dtypes.float8_e4m3fn).astype(np.float64)
    else:
        nib = np.empty((g, p, n, 4), np.uint8)
        nib[..., 0::2] = words & 0xF
        nib[..., 1::2] = words >> 4
        vals = E2M1[nib]
    vals = vals * np.repeat(np.exp2(scales.astype(np.float64) - 127.0), 8, axis=1)[..., None]
    return vals.transpose(0, 1, 3, 2).reshape(g * 512, n)

def pack4(w):
    words, scales = pack_weight(w, "e2m1")
    return words.reshape(words.shape[0], 128, -1), scales


def unpack4(words, scales):
    return unpack_weight(words.reshape(words.shape[0], 128, -1, 2), scales, "e2m1")


B, IN, OUT, G, P = 512, 1024, 1024, 5, 3
NB = G + P
LO, HI = -1.0, 1.0


def silu(v):
    return v / (1.0 + np.exp(-v))


def b_splines(x, grid):
    xe = x[..., None]
    bases = np.logical_and(xe >= grid[:, :-1], xe < grid[:, 1:]).astype(np.float64)
    for k in range(1, P + 1):
        left = (xe - grid[:, :-(k + 1)]) / (grid[:, k:-1] - grid[:, :-(k + 1)])
        right = (grid[:, k + 1:] - xe) / (grid[:, k + 1:] - grid[:, 1:-k])
        bases = left * bases[..., :-1] + right * bases[..., 1:]
    return bases


def setup_inputs():
    s = mx_kscale(IN)
    s = s / s.max()
    h = (HI - LO) / G
    g = np.arange(-P, G + P + 1) * h + LO
    x = bf(np.random.uniform(LO, HI, (B, IN)) * s)
    base = np.random.standard_normal((OUT, IN)) * 2.5 / np.sqrt(IN) / s[None, :]
    words, scales = pack4(np.ascontiguousarray(base.T))
    return {"x": x,
            "base_weight_words": words,
            "base_weight_scales": scales,
            "spline_weight": bf(np.random.standard_normal((OUT, IN, NB))),
            "spline_scaler": bf(np.random.standard_normal((OUT, IN)) * 1.5 / np.sqrt(IN)),
            "grid": bf(np.tile(g[None, :], (IN, 1)))}


def reference(x, base_weight_words, base_weight_scales, spline_weight, spline_scaler, grid):
    x, grid = f64(x), f64(grid)
    base_out = mxq(silu(x), 1, "e4m3") @ unpack4(base_weight_words, base_weight_scales)
    ssw = f64(spline_weight) * f64(spline_scaler)[..., None]
    bs = b_splines(x, grid).reshape(x.shape[0], -1)
    spline_out = mxq(bs, 1, "e4m3") @ mxq(ssw.reshape(OUT, -1), 1, "e4m3").T
    return base_out + spline_out

@@ -1,0 +1,245 @@
+from contextlib import ExitStack
+
+import concourse.bass as bass
+import concourse.mybir as mybir
+import concourse.tile as tile
+from concourse.masks import make_identity
+
+F32 = mybir.dt.float32
+BF16 = mybir.dt.bfloat16
+U8 = mybir.dt.uint8
+U32 = mybir.dt.uint32
+I32 = mybir.dt.int32
+FP8X4 = mybir.dt.float8_e4m3fn_x4
+FP4X4 = mybir.dt.float4_e2m1fn_x4
+ALU = mybir.AluOpType
+ACT = mybir.ActivationFunctionType
+
+P = 128
+B, IN, OUT, NB, KNOTS = 512, 1024, 1024, 8, 12
+CH = IN // P
+BT = B // P
+OT = OUT // P
+FLOPS = 2 * B * OUT * (IN * NB + IN)
+
+
+def tile_bsplinekanlayer_kernel(
+    tc, x, base_weight_words, base_weight_scales, spline_weight, spline_scaler, grid, out
+):
+    nc = tc.nc
+    with ExitStack() as ctx:
+        const = ctx.enter_context(tc.tile_pool(name="const", bufs=1))
+        swp = ctx.enter_context(tc.tile_pool(name="swp", bufs=4))
+        sws = ctx.enter_context(tc.tile_pool(name="sws", bufs=2))
+
+        ident_bf = const.tile([P, P], BF16)
+        make_identity(nc, ident_bf[:])
+        ident_f = const.tile([P, P], F32)
+        make_identity(nc, ident_f[:])
+        e2 = const.tile([P, P, 2], BF16)
+        nc.vector.tensor_copy(out=e2[:], in_=ident_bf[:].unsqueeze(2).to_broadcast([P, P, 2]))
+
+        knot = const.tile([P, CH, KNOTS], F32)
+        nknot = const.tile([P, CH, KNOTS], F32)
+        ca = const.tile([P, CH, 9], F32)
+        ce = const.tile([P, CH, 9], F32)
+        nbeta = const.tile([P, CH, 8], F32)
+        nphi = const.tile([P, CH, 8], F32)
+        xT = const.tile([P, CH, B], BF16)
+        sxc = const.tile([P, 2, B], U32, align_bytes=64)
+        sxs = const.tile([P, 2, B], U8, align_bytes=64)
+        wq = const.tile([P, 2, 2 * OUT], U8, align_bytes=64)
+        wsc = const.tile([P, 2, OUT], U8, align_bytes=64)
+        bsc = const.tile([P, 2 * CH, B], U32, align_bytes=64)
+        bss = const.tile([P, 2 * CH, B], U8, align_bytes=64)
+
+        nc.vector.memset(wsc[:].rearrange("p g n -> p (g n)").bitcast(I32), 0)
+
+        with tc.tile_pool(name="start", bufs=1) as st, tc.psum_pool(name="pstart", bufs=2) as ps0:
+            xs = st.tile([P, BT, IN], BF16)
+            nc.sync.dma_start(out=xs[:], in_=x.rearrange("(t p) i -> p t i", p=P))
+            graw = st.tile([P, CH, KNOTS], BF16)
+            nc.sync.dma_start(out=graw[:], in_=grid.rearrange("(c p) m -> p c m", p=P))
+            for g in range(2):
+                for q in range(4):
+                    nc.sync.dma_start(
+                        out=wsc[32 * q : 32 * q + 4, g, :].bitcast(I32),
+                        in_=base_weight_scales[g, 4 * q : 4 * q + 4, :].bitcast(I32),
+                    )
+            for g in range(2):
+                nc.sync.dma_start(out=wq[:, g, :].bitcast(I32), in_=base_weight_words[g].bitcast(I32))
+
+            nc.vector.tensor_copy(out=knot[:], in_=graw[:])
+            nc.vector.tensor_scalar(out=nknot[:], in0=knot[:], scalar1=-1.0, scalar2=None, op0=ALU.mult)
+            d1 = st.tile([P, CH, 11], F32)
+            d2 = st.tile([P, CH, 10], F32)
+            d3 = st.tile([P, CH, 9], F32)
+            d4 = st.tile([P, CH, 8], F32)
+            r1 = st.tile([P, CH, 11], F32)
+            pa = st.tile([P, CH, 9], F32)
+            pe = st.tile([P, CH, 9], F32)
+            nc.vector.tensor_tensor(out=d1[:], in0=knot[:, :, 1:12], in1=knot[:, :, 0:11], op=ALU.subtract)
+            nc.vector.tensor_tensor(out=d2[:], in0=knot[:, :, 2:12], in1=knot[:, :, 0:10], op=ALU.subtract)
+            nc.vector.tensor_tensor(out=d3[:], in0=knot[:, :, 3:12], in1=knot[:, :, 0:9], op=ALU.subtract)
+            nc.vector.tensor_tensor(out=d4[:], in0=knot[:, :, 4:12], in1=knot[:, :, 0:8], op=ALU.subtract)
+            nc.vector.tensor_tensor(out=pa[:], in0=d1[:, :, 0:9], in1=d2[:, :, 0:9], op=ALU.mult)
+            nc.vector.tensor_tensor(out=pa[:], in0=pa[:], in1=d3[:], op=ALU.mult)
+            nc.vector.reciprocal(out=ca[:], in_=pa[:])
+            nc.vector.tensor_tensor(out=pe[:], in0=d1[:, :, 2:11], in1=d2[:, :, 1:10], op=ALU.mult)
+            nc.vector.tensor_tensor(out=pe[:], in0=pe[:], in1=d3[:], op=ALU.mult)
+            nc.vector.reciprocal(out=pe[:], in_=pe[:])
+            nc.vector.tensor_scalar(out=ce[:], in0=pe[:], scalar1=-1.0, scalar2=None, op0=ALU.mult)
+            nc.vector.reciprocal(out=r1[:], in_=d1[:])
+            nc.vector.scalar_tensor_tensor(
+                out=nbeta[:], in0=d4[:], scalar=-1.0, in1=r1[:, :, 0:8], op0=ALU.mult, op1=ALU.mult
+            )
+            nc.vector.scalar_tensor_tensor(
+                out=nphi[:], in0=d4[:], scalar=-1.0, in1=r1[:, :, 3:11], op0=ALU.mult, op1=ALU.mult
+            )
+
+            for c2 in range(CH // 2):
+                ptx = ps0.tile([P, 2, B], BF16)
+                for cc in range(2):
+                    c = 2 * c2 + cc
+                    for t in range(BT):
+                        nc.tensor.transpose(
+                            ptx[:, cc, t * P : (t + 1) * P], xs[:, t, c * P : (c + 1) * P], ident_bf[:]
+                        )
+                nc.scalar.copy(out=xT[:, 2 * c2 : 2 * c2 + 2, :], in_=ptx[:])
+
+            sg = st.tile([P, 2, 4 * B], BF16, align_bytes=64)
+            for g in range(2):
+                for hb in range(2):
+                    pw = ps0.tile([P, 2, 2 * P], F32)
+                    for u in range(2):
+                        for t2 in range(2):
+                            t = 2 * hb + t2
+                            nc.tensor.transpose(
+                                pw[:, u, t2 * P : (t2 + 1) * P],
+                                xs[:, t, :].bitcast(F32)[:, 256 * g + u : 256 * (g + 1) : 2],
+                                ident_f[:],
+                            )
+                    nc.scalar.activation(
+                        out=sg[:, g, hb * 1024 : (hb + 1) * 1024].rearrange("p (b u e) -> p b u e", u=2, e=2),
+                        in_=pw[:].bitcast(BF16).rearrange("p u (b e) -> p b u e", e=2),
+                        func=ACT.Silu,
+                    )
+            nc.vector.quantize_mx(
+                out=sxc[:].rearrange("p g n -> p (g n)").bitcast(FP8X4),
+                scales=sxs[:].rearrange("p g n -> p (g n)"),
+                in_=sg[:].rearrange("p g n -> p (g n)"),
+            )
+
+        pswt = ctx.enter_context(tc.psum_pool(name="pswt", bufs=4))
+        psc = ctx.enter_context(tc.psum_pool(name="psc", bufs=2))
+        pacc = ctx.enter_context(tc.psum_pool(name="pacc", bufs=2))
+
+        with tc.tile_pool(name="work", bufs=3) as wk:
+            for c in range(CH):
+                v = xT[:, c, :]
+                apl = wk.tile([P, NB, B], BF16, bufs=2)
+                bpl = wk.tile([P, NB, B], BF16, bufs=2)
+                ras = {}
+                las = {}
+                for m in range(KNOTS):
+                    sq = wk.tile([P, B], F32)
+                    nc.scalar.activation(out=sq[:], in_=v, func=ACT.Square, bias=nknot[:, c, m : m + 1], scale=1.0)
+                    z = wk.tile([P, B], F32)
+                    nc.vector.scalar_tensor_tensor(
+                        out=z[:], in0=v, scalar=knot[:, c, m : m + 1], in1=sq[:], op0=ALU.subtract, op1=ALU.mult
+                    )
+                    if m <= 8:
+                        ra = wk.tile([P, B], F32, bufs=4)
+                        nc.scalar.activation(out=ra[:], in_=z[:], func=ACT.Relu, scale=ca[:, c, m : m + 1])
+                        ras[m] = ra
+                    if m >= 3:
+                        la = wk.tile([P, B], F32, bufs=4)
+                        nc.scalar.activation(out=la[:], in_=z[:], func=ACT.Relu, scale=ce[:, c, m - 3 : m - 2])
+                        las[m] = la
+                    if 1 <= m <= 8:
+                        j = m - 1
+                        nc.vector.scalar_tensor_tensor(
+                            out=apl[:, j, :], in0=ras[m][:], scalar=nbeta[:, c, j : j + 1], in1=ras[m - 1][:],
+                            op0=ALU.mult, op1=ALU.add,
+                        )
+                    if m >= 4:
+                        j = m - 4
+                        nc.vector.scalar_tensor_tensor(
+                            out=bpl[:, j, :], in0=las[m - 1][:], scalar=nphi[:, c, j : j + 1], in1=las[m][:],
+                            op0=ALU.mult, op1=ALU.add,
+                        )
+                nc.vector.tensor_tensor(out=apl[:], in0=apl[:], in1=bpl[:], op=ALU.max)
+                grp = wk.tile([P, 2, B, 4], BF16, bufs=2, align_bytes=64)
+                for h in range(2):
+                    nc.vector.tensor_copy(
+                        out=grp[:, h].rearrange("p (c i) t -> p c t i", i=4),
+                        in_=apl[:, 4 * h : 4 * h + 4, :].rearrange("p t (c i) -> p c t i", i=4),
+                    )
+                nc.vector.quantize_mx(
+                    out=bsc[:, 2 * c : 2 * c + 2, :].rearrange("p a n -> p (a n)").bitcast(FP8X4),
+                    scales=bss[:, 2 * c : 2 * c + 2, :].rearrange("p a n -> p (a n)"),
+                    in_=grp[:].rearrange("p h b t -> p (h b t)"),
+                )
+
+        out_v = out.rearrange("(t p) o -> p t o", p=P)
+        for ot in range(OT):
+            rows = slice(ot * P, (ot + 1) * P)
+            sct = sws.tile([P, IN], BF16)
+            nc.sync.dma_start(out=sct[:], in_=spline_scaler[rows, :])
+            sc2 = sws.tile([P, CH, 2 * P], BF16)
+            for c4 in range(2):
+                pq = psc.tile([P, 4, 2 * P], BF16)
+                for cl in range(4):
+                    c = 4 * c4 + cl
+                    nc.tensor.matmul(
+                        out=pq[:, cl, :], lhsT=sct[:, c * P : (c + 1) * P],
+                        rhs=e2[:].rearrange("p o e -> p (o e)"), start=True, stop=True,
+                    )
+                nc.scalar.copy(out=sc2[:, 4 * c4 : 4 * c4 + 4, :], in_=pq[:])
+            sswc = sws.tile([P, 2 * CH, P], U32, bufs=3, align_bytes=64)
+            ssws = sws.tile([P, 2 * CH, P], U8, bufs=3, align_bytes=64)
+            for hf in range(2):
+                swt = swp.tile([P, 4 * P * NB], BF16)
+                nc.sync.dma_start(
+                    out=swt[:],
+                    in_=spline_weight[rows, hf * 512 : (hf + 1) * 512, :].rearrange("o i j -> o (i j)"),
+                )
+                sww = swt[:].bitcast(F32)
+                for cl in range(4):
+                    c = 4 * hf + cl
+                    bank = pswt.tile([P, 4, P], F32)
+                    for jj in range(4):
+                        nc.tensor.transpose(bank[:, jj, :], sww[:, 512 * cl + jj : 512 * (cl + 1) : 4], ident_f[:])
+                    gt = sws.tile([P, 2, 4 * P], BF16, bufs=4, align_bytes=64)
+                    bview = bank[:].bitcast(BF16).rearrange("p (h u) (o e) -> p h o u e", u=2, e=2)
+                    sview = sc2[:, c, :].rearrange("p (o e) -> p o e", e=2).unsqueeze(2).to_broadcast([P, P, 2, 2])
+                    for h in range(2):
+                        nc.vector.tensor_tensor(
+                            out=gt[:, h, :].rearrange("p (o u e) -> p o u e", u=2, e=2),
+                            in0=bview[:, h], in1=sview, op=ALU.mult,
+                        )
+                    nc.vector.quantize_mx(
+                        out=sswc[:, 2 * c : 2 * c + 2, :].rearrange("p a n -> p (a n)").bitcast(FP8X4),
+                        scales=ssws[:, 2 * c : 2 * c + 2, :].rearrange("p a n -> p (a n)"),
+                        in_=gt[:].rearrange("p h n -> p (h n)"),
+                    )
+            acc = pacc.tile([P, BT, P], F32)
+            for t in range(BT):
+                cols = slice(t * P, (t + 1) * P)
+                for g in range(2):
+                    nc.tensor.matmul_mx(
+                        out=acc[:, t, :],
+                        lhsT=sxc[:, g, cols].bitcast(FP8X4), lhsT_scale=sxs[:, g, cols],
+                        rhs=wq[:, g, ot * 2 * P : (ot + 1) * 2 * P].bitcast(FP4X4), rhs_scale=wsc[:, g, rows],
+                        start=(g == 0), stop=False,
+                    )
+                for ps in range(2 * CH):
+                    nc.tensor.matmul_mx(
+                        out=acc[:, t, :],
+                        lhsT=bsc[:, ps, cols].bitcast(FP8X4), lhsT_scale=bss[:, ps, cols],
+                        rhs=sswc[:, ps, :].bitcast(FP8X4), rhs_scale=ssws[:, ps, :],
+                        start=False, stop=(ps == 2 * CH - 1),
+                    )
+            res = sws.tile([P, BT, P], F32)
+            nc.scalar.copy(out=res[:], in_=acc[:])
+            nc.sync.dma_start(out=out_v[:, :, rows], in_=res[:])

@@ -1,8 +1,6 @@
 from contextlib import ExitStack
 
-import concourse.bass as bass
 import concourse.mybir as mybir
-import concourse.tile as tile
 from concourse.masks import make_identity
 
 F32 = mybir.dt.float32
@@ -21,6 +19,8 @@ CH = IN // P
 BT = B // P
 OT = OUT // P
 FLOPS = 2 * B * OUT * (IN * NB + IN)
+EARLY = 5
+V_REGROUP = ((5, 0), (6, 0), (7, 0), (7, 1))
 
 
 def tile_bsplinekanlayer_kernel(
@@ -29,8 +29,6 @@ def tile_bsplinekanlayer_kernel(
     nc = tc.nc
     with ExitStack() as ctx:
         const = ctx.enter_context(tc.tile_pool(name="const", bufs=1))
-        swp = ctx.enter_context(tc.tile_pool(name="swp", bufs=4))
-        sws = ctx.enter_context(tc.tile_pool(name="sws", bufs=2))
 
         ident_bf = const.tile([P, P], BF16)
         make_identity(nc, ident_bf[:])
@@ -50,8 +48,13 @@ def tile_bsplinekanlayer_kernel(
         sxs = const.tile([P, 2, B], U8, align_bytes=64)
         wq = const.tile([P, 2, 2 * OUT], U8, align_bytes=64)
         wsc = const.tile([P, 2, OUT], U8, align_bytes=64)
-        bsc = const.tile([P, 2 * CH, B], U32, align_bytes=64)
-        bss = const.tile([P, 2 * CH, B], U8, align_bytes=64)
+        sswc = const.tile([P, 2 * CH, OUT], U32, align_bytes=64)
+        ssws = const.tile([P, 2 * CH, OUT], U8, align_bytes=64)
+        bsc = {}
+        bss = {}
+        for c in range(EARLY):
+            bsc[c] = const.tile([P, 2, B], U32, align_bytes=64, name="bsc%d" % c)
+            bss[c] = const.tile([P, 2, B], U8, align_bytes=64, name="bss%d" % c)
 
         nc.vector.memset(wsc[:].rearrange("p g n -> p (g n)").bitcast(I32), 0)
 
@@ -60,14 +63,6 @@ def tile_bsplinekanlayer_kernel(
             nc.sync.dma_start(out=xs[:], in_=x.rearrange("(t p) i -> p t i", p=P))
             graw = st.tile([P, CH, KNOTS], BF16)
             nc.sync.dma_start(out=graw[:], in_=grid.rearrange("(c p) m -> p c m", p=P))
-            for g in range(2):
-                for q in range(4):
-                    nc.sync.dma_start(
-                        out=wsc[32 * q : 32 * q + 4, g, :].bitcast(I32),
-                        in_=base_weight_scales[g, 4 * q : 4 * q + 4, :].bitcast(I32),
-                    )
-            for g in range(2):
-                nc.sync.dma_start(out=wq[:, g, :].bitcast(I32), in_=base_weight_words[g].bitcast(I32))
 
             nc.vector.tensor_copy(out=knot[:], in_=graw[:])
             nc.vector.tensor_scalar(out=nknot[:], in0=knot[:], scalar1=-1.0, scalar2=None, op0=ALU.mult)
@@ -130,116 +125,172 @@ def tile_bsplinekanlayer_kernel(
                 in_=sg[:].rearrange("p g n -> p (g n)"),
             )
 
-        pswt = ctx.enter_context(tc.psum_pool(name="pswt", bufs=4))
-        psc = ctx.enter_context(tc.psum_pool(name="psc", bufs=2))
-        pacc = ctx.enter_context(tc.psum_pool(name="pacc", bufs=2))
+        wk = ctx.enter_context(tc.tile_pool(name="work", bufs=3))
+        live = {}
 
-        with tc.tile_pool(name="work", bufs=3) as wk:
-            for c in range(CH):
-                v = xT[:, c, :]
-                apl = wk.tile([P, NB, B], BF16, bufs=2)
-                bpl = wk.tile([P, NB, B], BF16, bufs=2)
-                ras = {}
-                las = {}
-                for m in range(KNOTS):
-                    sq = wk.tile([P, B], F32)
-                    nc.scalar.activation(out=sq[:], in_=v, func=ACT.Square, bias=nknot[:, c, m : m + 1], scale=1.0)
-                    z = wk.tile([P, B], F32)
-                    nc.vector.scalar_tensor_tensor(
-                        out=z[:], in0=v, scalar=knot[:, c, m : m + 1], in1=sq[:], op0=ALU.subtract, op1=ALU.mult
+        def bs_step(c, m):
+            v = xT[:, c, :]
+            sq = wk.tile([P, B], F32, name="sq")
+            nc.scalar.activation(out=sq[:], in_=v, func=ACT.Square, bias=nknot[:, c, m : m + 1], scale=1.0)
+            z = wk.tile([P, B], F32, name="z")
+            nc.vector.scalar_tensor_tensor(
+                out=z[:], in0=v, scalar=knot[:, c, m : m + 1], in1=sq[:], op0=ALU.subtract, op1=ALU.mult
+            )
+            if m <= 8:
+                ra = wk.tile([P, B], F32, bufs=4, name="ra")
+                nc.scalar.activation(out=ra[:], in_=z[:], func=ACT.Relu, scale=ca[:, c, m : m + 1])
+                live[("ra", m)] = ra
+            if m >= 3:
+                la = wk.tile([P, B], F32, bufs=4, name="la")
+                nc.scalar.activation(out=la[:], in_=z[:], func=ACT.Relu, scale=ce[:, c, m - 3 : m - 2])
+                live[("la", m)] = la
+            if 1 <= m <= 8:
+                j = m - 1
+                if j % 4 == 0:
+                    live[("apl", j // 4)] = wk.tile([P, 4, B], BF16, name="apl")
+                nc.vector.scalar_tensor_tensor(
+                    out=live[("apl", j // 4)][:, j % 4, :], in0=live[("ra", m)][:], scalar=nbeta[:, c, j : j + 1],
+                    in1=live[("ra", m - 1)][:], op0=ALU.mult, op1=ALU.add,
+                )
+            if m >= 4:
+                j = m - 4
+                if j % 4 == 0:
+                    live[("bpl", j // 4)] = wk.tile([P, 4, B], BF16, name="bpl")
+                nc.vector.scalar_tensor_tensor(
+                    out=live[("bpl", j // 4)][:, j % 4, :], in0=live[("la", m - 1)][:], scalar=nphi[:, c, j : j + 1],
+                    in1=live[("la", m)][:], op0=ALU.mult, op1=ALU.add,
+                )
+                if j % 4 == 3:
+                    bs_finish(c, j // 4)
+
+        def bs_finish(c, h):
+            apl = live[("apl", h)]
+            nc.vector.tensor_tensor(out=apl[:], in0=apl[:], in1=live[("bpl", h)][:], op=ALU.max)
+            grp = wk.tile([P, B, 4], BF16, align_bytes=64, name="grp")
+            dst = grp[:].rearrange("p (c i) t -> p c t i", i=4)
+            src = apl[:].rearrange("p t (c i) -> p c t i", i=4)
+            if (c, h) in V_REGROUP:
+                nc.vector.tensor_copy(out=dst, in_=src)
+            else:
+                nc.scalar.copy(out=dst, in_=src)
+            nc.vector.quantize_mx(
+                out=bsc[c][:, h, :].bitcast(FP8X4), scales=bss[c][:, h, :], in_=grp[:].rearrange("p b t -> p (b t)")
+            )
+
+        with tc.tile_pool(name="swp", bufs=4) as swp, tc.tile_pool(name="sws", bufs=3) as sws, tc.psum_pool(
+            name="pswt", bufs=4
+        ) as pswt, tc.psum_pool(name="psc", bufs=2) as psc:
+            for g in range(2):
+                for q in range(4):
+                    nc.sync.dma_start(
+                        out=wsc[32 * q : 32 * q + 4, g, :].bitcast(I32),
+                        in_=base_weight_scales[g, 4 * q : 4 * q + 4, :].bitcast(I32),
                     )
-                    if m <= 8:
-                        ra = wk.tile([P, B], F32, bufs=4)
-                        nc.scalar.activation(out=ra[:], in_=z[:], func=ACT.Relu, scale=ca[:, c, m : m + 1])
-                        ras[m] = ra
-                    if m >= 3:
-                        la = wk.tile([P, B], F32, bufs=4)
-                        nc.scalar.activation(out=la[:], in_=z[:], func=ACT.Relu, scale=ce[:, c, m - 3 : m - 2])
-                        las[m] = la
-                    if 1 <= m <= 8:
-                        j = m - 1
-                        nc.vector.scalar_tensor_tensor(
-                            out=apl[:, j, :], in0=ras[m][:], scalar=nbeta[:, c, j : j + 1], in1=ras[m - 1][:],
-                            op0=ALU.mult, op1=ALU.add,
+            for g in range(2):
+                nc.sync.dma_start(out=wq[:, g, :].bitcast(I32), in_=base_weight_words[g].bitcast(I32))
+
+            def ssw_unit(ot, c):
+                rows = slice(ot * P, (ot + 1) * P)
+                if c == 0:
+                    sct = sws.tile([P, IN], BF16, bufs=2, name="sct")
+                    nc.sync.dma_start(out=sct[:], in_=spline_scaler[rows, :])
+                    live["sct"] = sct
+                if c % 4 == 0:
+                    pq = psc.tile([P, 4, 2 * P], BF16, name="pq")
+                    for cl in range(4):
+                        nc.tensor.matmul(
+                            out=pq[:, cl, :], lhsT=live["sct"][:, (c + cl) * P : (c + cl + 1) * P],
+                            rhs=e2[:].rearrange("p o e -> p (o e)"), start=True, stop=True,
                         )
-                    if m >= 4:
-                        j = m - 4
-                        nc.vector.scalar_tensor_tensor(
-                            out=bpl[:, j, :], in0=las[m - 1][:], scalar=nphi[:, c, j : j + 1], in1=las[m][:],
-                            op0=ALU.mult, op1=ALU.add,
-                        )
-                nc.vector.tensor_tensor(out=apl[:], in0=apl[:], in1=bpl[:], op=ALU.max)
-                grp = wk.tile([P, 2, B, 4], BF16, bufs=2, align_bytes=64)
+                    sc2 = sws.tile([P, 4, 2, 2 * P], BF16, name="sc2")
+                    nc.scalar.copy(out=sc2[:], in_=pq[:].unsqueeze(2).to_broadcast([P, 4, 2, 2 * P]))
+                    live["sc2"] = sc2
+                if c % 2 == 0:
+                    swt = swp.tile([P, 2 * P * NB], BF16, name="swt")
+                    nc.sync.dma_start(
+                        out=swt[:],
+                        in_=spline_weight[rows, c * P : (c + 2) * P, :].rearrange("o i j -> o (i j)"),
+                    )
+                    live["swt"] = swt
+                sww = live["swt"][:].bitcast(F32)
+                cl = c % 2
+                bank = pswt.tile([P, 4, P], F32, name="bank")
+                for jj in range(4):
+                    nc.tensor.transpose(
+                        bank[:, (jj % 2) * 2 + jj // 2, :], sww[:, 512 * cl + jj : 512 * (cl + 1) : 4], ident_f[:]
+                    )
+                gt = sws.tile([P, 8 * P], BF16, align_bytes=64, name="gt")
+                nc.vector.tensor_tensor(
+                    out=gt[:].rearrange("p (q u e) -> p q u e", u=2, e=2),
+                    in0=bank[:].rearrange("p a o -> p (a o)").bitcast(BF16).rearrange("p (u q e) -> p q u e", u=2, e=2),
+                    in1=live["sc2"][:, c % 4].rearrange("p h n -> p (h n)").rearrange("p (q e) -> p q e", e=2)
+                    .unsqueeze(2).to_broadcast([P, 2 * P, 2, 2]),
+                    op=ALU.mult,
+                )
                 for h in range(2):
-                    nc.vector.tensor_copy(
-                        out=grp[:, h].rearrange("p (c i) t -> p c t i", i=4),
-                        in_=apl[:, 4 * h : 4 * h + 4, :].rearrange("p t (c i) -> p c t i", i=4),
-                    )
-                nc.vector.quantize_mx(
-                    out=bsc[:, 2 * c : 2 * c + 2, :].rearrange("p a n -> p (a n)").bitcast(FP8X4),
-                    scales=bss[:, 2 * c : 2 * c + 2, :].rearrange("p a n -> p (a n)"),
-                    in_=grp[:].rearrange("p h b t -> p (h b t)"),
-                )
-
-        out_v = out.rearrange("(t p) o -> p t o", p=P)
-        for ot in range(OT):
-            rows = slice(ot * P, (ot + 1) * P)
-            sct = sws.tile([P, IN], BF16)
-            nc.sync.dma_start(out=sct[:], in_=spline_scaler[rows, :])
-            sc2 = sws.tile([P, CH, 2 * P], BF16)
-            for c4 in range(2):
-                pq = psc.tile([P, 4, 2 * P], BF16)
-                for cl in range(4):
-                    c = 4 * c4 + cl
-                    nc.tensor.matmul(
-                        out=pq[:, cl, :], lhsT=sct[:, c * P : (c + 1) * P],
-                        rhs=e2[:].rearrange("p o e -> p (o e)"), start=True, stop=True,
-                    )
-                nc.scalar.copy(out=sc2[:, 4 * c4 : 4 * c4 + 4, :], in_=pq[:])
-            sswc = sws.tile([P, 2 * CH, P], U32, bufs=3, align_bytes=64)
-            ssws = sws.tile([P, 2 * CH, P], U8, bufs=3, align_bytes=64)
-            for hf in range(2):
-                swt = swp.tile([P, 4 * P * NB], BF16)
-                nc.sync.dma_start(
-                    out=swt[:],
-                    in_=spline_weight[rows, hf * 512 : (hf + 1) * 512, :].rearrange("o i j -> o (i j)"),
-                )
-                sww = swt[:].bitcast(F32)
-                for cl in range(4):
-                    c = 4 * hf + cl
-                    bank = pswt.tile([P, 4, P], F32)
-                    for jj in range(4):
-                        nc.tensor.transpose(bank[:, jj, :], sww[:, 512 * cl + jj : 512 * (cl + 1) : 4], ident_f[:])
-                    gt = sws.tile([P, 2, 4 * P], BF16, bufs=4, align_bytes=64)
-                    bview = bank[:].bitcast(BF16).rearrange("p (h u) (o e) -> p h o u e", u=2, e=2)
-                    sview = sc2[:, c, :].rearrange("p (o e) -> p o e", e=2).unsqueeze(2).to_broadcast([P, P, 2, 2])
-                    for h in range(2):
-                        nc.vector.tensor_tensor(
-                            out=gt[:, h, :].rearrange("p (o u e) -> p o u e", u=2, e=2),
-                            in0=bview[:, h], in1=sview, op=ALU.mult,
-                        )
                     nc.vector.quantize_mx(
-                        out=sswc[:, 2 * c : 2 * c + 2, :].rearrange("p a n -> p (a n)").bitcast(FP8X4),
-                        scales=ssws[:, 2 * c : 2 * c + 2, :].rearrange("p a n -> p (a n)"),
-                        in_=gt[:].rearrange("p h n -> p (h n)"),
+                        out=sswc[:, 2 * c + h, rows].bitcast(FP8X4), scales=ssws[:, 2 * c + h, rows],
+                        in_=gt[:, h * 4 * P : (h + 1) * 4 * P],
                     )
-            acc = pacc.tile([P, BT, P], F32)
+
+            units = [(ot, c) for ot in range(OT) for c in range(CH)]
+            steps = EARLY * KNOTS
+            done = 0
+            for s in range(steps):
+                bs_step(s // KNOTS, s % KNOTS)
+                want = ((s + 1) * len(units) + steps - 1) // steps
+                while done < min(want, len(units)):
+                    ssw_unit(units[done][0], units[done][1])
+                    done += 1
+
+        pacc = ctx.enter_context(tc.psum_pool(name="pacc", bufs=1))
+        late = ctx.enter_context(tc.tile_pool(name="late", bufs=1))
+        acc = {}
+        for t in range(BT):
+            for oh in range(2):
+                acc[(t, oh)] = pacc.tile([P, 512], F32, name="acc%d%d" % (t, oh))
+        for g in range(2):
             for t in range(BT):
-                cols = slice(t * P, (t + 1) * P)
-                for g in range(2):
+                for oh in range(2):
                     nc.tensor.matmul_mx(
-                        out=acc[:, t, :],
-                        lhsT=sxc[:, g, cols].bitcast(FP8X4), lhsT_scale=sxs[:, g, cols],
-                        rhs=wq[:, g, ot * 2 * P : (ot + 1) * 2 * P].bitcast(FP4X4), rhs_scale=wsc[:, g, rows],
+                        out=acc[(t, oh)][:],
+                        lhsT=sxc[:, g, t * P : (t + 1) * P].bitcast(FP8X4), lhsT_scale=sxs[:, g, t * P : (t + 1) * P],
+                        rhs=wq[:, g, oh * 1024 : (oh + 1) * 1024].bitcast(FP4X4),
+                        rhs_scale=wsc[:, g, oh * 512 : (oh + 1) * 512],
                         start=(g == 0), stop=False,
                     )
-                for ps in range(2 * CH):
+
+        def mx_passes(c, h):
+            for t in range(BT):
+                for oh in range(2):
                     nc.tensor.matmul_mx(
-                        out=acc[:, t, :],
-                        lhsT=bsc[:, ps, cols].bitcast(FP8X4), lhsT_scale=bss[:, ps, cols],
-                        rhs=sswc[:, ps, :].bitcast(FP8X4), rhs_scale=ssws[:, ps, :],
-                        start=False, stop=(ps == 2 * CH - 1),
+                        out=acc[(t, oh)][:],
+                        lhsT=bsc[c][:, h, t * P : (t + 1) * P].bitcast(FP8X4),
+                        lhsT_scale=bss[c][:, h, t * P : (t + 1) * P],
+                        rhs=sswc[:, 2 * c + h, oh * 512 : (oh + 1) * 512].bitcast(FP8X4),
+                        rhs_scale=ssws[:, 2 * c + h, oh * 512 : (oh + 1) * 512],
+                        start=False, stop=(c == CH - 1 and h == 1),
                     )
-            res = sws.tile([P, BT, P], F32)
-            nc.scalar.copy(out=res[:], in_=acc[:])
-            nc.sync.dma_start(out=out_v[:, :, rows], in_=res[:])
+
+        for c in range(EARLY):
+            mx_passes(c, 0)
+            mx_passes(c, 1)
+        for c in range(EARLY, CH):
+            bsc[c] = late.tile([P, 2, B], U32, align_bytes=64, name="bsc%d" % c)
+            bss[c] = late.tile([P, 2, B], U8, align_bytes=64, name="bss%d" % c)
+            for m in range(KNOTS):
+                bs_step(c, m)
+                if m == 9:
+                    mx_passes(c, 0)
+            mx_passes(c, 1)
+
+        n = 0
+        for t in range(BT):
+            for oh in range(2):
+                res = late.tile([P, 512], F32, bufs=4, name="res")
+                if n % 2 == 0:
+                    nc.scalar.copy(out=res[:], in_=acc[(t, oh)][:])
+                else:
+                    nc.vector.tensor_copy(out=res[:], in_=acc[(t, oh)][:])
+                nc.sync.dma_start(out=out[t * P : (t + 1) * P, oh * 512 : (oh + 1) * 512], in_=res[:])
+                n += 1

@@ -19,8 +19,8 @@ CH = IN // P
 BT = B // P
 OT = OUT // P
 FLOPS = 2 * B * OUT * (IN * NB + IN)
-EARLY = 5
-V_REGROUP = ((5, 0), (6, 0), (7, 0), (7, 1))
+EARLY = 6
+V_REGROUP = ((7, 1),)
 
 
 def tile_bsplinekanlayer_kernel(
@@ -100,7 +100,7 @@ def tile_bsplinekanlayer_kernel(
                         nc.tensor.transpose(
                             ptx[:, cc, t * P : (t + 1) * P], xs[:, t, c * P : (c + 1) * P], ident_bf[:]
                         )
-                nc.scalar.copy(out=xT[:, 2 * c2 : 2 * c2 + 2, :], in_=ptx[:])
+                nc.vector.tensor_copy(out=xT[:, 2 * c2 : 2 * c2 + 2, :], in_=ptx[:])
 
             sg = st.tile([P, 2, 4 * B], BF16, align_bytes=64)
             for g in range(2):
@@ -177,7 +177,7 @@ def tile_bsplinekanlayer_kernel(
                 out=bsc[c][:, h, :].bitcast(FP8X4), scales=bss[c][:, h, :], in_=grp[:].rearrange("p b t -> p (b t)")
             )
 
-        with tc.tile_pool(name="swp", bufs=4) as swp, tc.tile_pool(name="sws", bufs=3) as sws, tc.psum_pool(
+        with tc.tile_pool(name="swp", bufs=3) as swp, tc.tile_pool(name="sws", bufs=3) as sws, tc.psum_pool(
             name="pswt", bufs=4
         ) as pswt, tc.psum_pool(name="psc", bufs=2) as psc:
             for g in range(2):

@@ -21,6 +21,7 @@ OT = OUT // P
 FLOPS = 2 * B * OUT * (IN * NB + IN)
 EARLY = 6
 V_REGROUP = ((7, 1),)
+FIRST = 8
 
 
 def tile_bsplinekanlayer_kernel(
@@ -34,6 +35,8 @@ def tile_bsplinekanlayer_kernel(
         make_identity(nc, ident_bf[:])
         ident_f = const.tile([P, P], F32)
         make_identity(nc, ident_f[:])
+        warm = const.tile([P, 1], F32)
+        nc.scalar.activation(out=warm[:], in_=ident_f[:, 0:1], func=ACT.Silu)
         e2 = const.tile([P, P, 2], BF16)
         nc.vector.tensor_copy(out=e2[:], in_=ident_bf[:].unsqueeze(2).to_broadcast([P, P, 2]))
 
@@ -58,11 +61,91 @@ def tile_bsplinekanlayer_kernel(
 
         nc.vector.memset(wsc[:].rearrange("p g n -> p (g n)").bitcast(I32), 0)
 
+        wk = ctx.enter_context(tc.tile_pool(name="work", bufs=3))
+        live = {}
+
+        def st_sq(c, m):
+            sq = wk.tile([P, B], F32, bufs=4, name="sq")
+            nc.scalar.activation(out=sq[:], in_=xT[:, c, :], func=ACT.Square, bias=nknot[:, c, m : m + 1], scale=1.0)
+            live[("sq", c, m)] = sq
+
+        def st_z(c, m):
+            z = wk.tile([P, B], F32, bufs=4, name="z")
+            nc.vector.scalar_tensor_tensor(
+                out=z[:], in0=xT[:, c, :], scalar=knot[:, c, m : m + 1], in1=live[("sq", c, m)][:],
+                op0=ALU.subtract, op1=ALU.mult,
+            )
+            live[("z", c, m)] = z
+
+        def st_relu(c, m):
+            z = live[("z", c, m)]
+            if m <= 8:
+                ra = wk.tile([P, B], F32, bufs=5, name="ra")
+                nc.scalar.activation(out=ra[:], in_=z[:], func=ACT.Relu, scale=ca[:, c, m : m + 1])
+                live[("ra", c, m)] = ra
+            if m >= 3:
+                la = wk.tile([P, B], F32, bufs=5, name="la")
+                nc.scalar.activation(out=la[:], in_=z[:], func=ACT.Relu, scale=ce[:, c, m - 3 : m - 2])
+                live[("la", c, m)] = la
+
+        def st_ab(c, m):
+            if 1 <= m <= 8:
+                j = m - 1
+                if j % 4 == 0:
+                    live[("apl", j // 4)] = wk.tile([P, 4, B], BF16, bufs=2, name="apl")
+                nc.vector.scalar_tensor_tensor(
+                    out=live[("apl", j // 4)][:, j % 4, :], in0=live[("ra", c, m)][:], scalar=nbeta[:, c, j : j + 1],
+                    in1=live[("ra", c, m - 1)][:], op0=ALU.mult, op1=ALU.add,
+                )
+            if m >= 4:
+                j = m - 4
+                if j % 4 == 0:
+                    live[("bpl", j // 4)] = wk.tile([P, 4, B], BF16, bufs=2, name="bpl")
+                nc.vector.scalar_tensor_tensor(
+                    out=live[("bpl", j // 4)][:, j % 4, :], in0=live[("la", c, m - 1)][:], scalar=nphi[:, c, j : j + 1],
+                    in1=live[("la", c, m)][:], op0=ALU.mult, op1=ALU.add,
+                )
+                if j % 4 == 3:
+                    bs_finish(c, j // 4)
+
+        def bs_step(c, m):
+            s = c * KNOTS + m
+            if s == 0:
+                st_sq(0, 0)
+                st_sq(0, 1)
+                st_sq(0, 2)
+                st_z(0, 0)
+                st_z(0, 1)
+                st_relu(0, 0)
+            if s + 3 < CH * KNOTS:
+                st_sq((s + 3) // KNOTS, (s + 3) % KNOTS)
+            if s + 2 < CH * KNOTS:
+                st_z((s + 2) // KNOTS, (s + 2) % KNOTS)
+            if s + 1 < CH * KNOTS:
+                st_relu((s + 1) // KNOTS, (s + 1) % KNOTS)
+            st_ab(c, m)
+
+        def bs_finish(c, h):
+            apl = live[("apl", h)]
+            nc.vector.tensor_tensor(out=apl[:], in0=apl[:], in1=live[("bpl", h)][:], op=ALU.max)
+            grp = wk.tile([P, B, 4], BF16, bufs=2, align_bytes=64, name="grp")
+            dst = grp[:].rearrange("p (c i) t -> p c t i", i=4)
+            src = apl[:].rearrange("p t (c i) -> p c t i", i=4)
+            if (c, h) in V_REGROUP:
+                nc.vector.tensor_copy(out=dst, in_=src)
+            else:
+                nc.scalar.copy(out=dst, in_=src)
+            nc.vector.quantize_mx(
+                out=bsc[c][:, h, :].bitcast(FP8X4), scales=bss[c][:, h, :], in_=grp[:].rearrange("p b t -> p (b t)")
+            )
+
         with tc.tile_pool(name="start", bufs=1) as st, tc.psum_pool(name="pstart", bufs=2) as ps0:
-            xs = st.tile([P, BT, IN], BF16)
-            nc.sync.dma_start(out=xs[:], in_=x.rearrange("(t p) i -> p t i", p=P))
             graw = st.tile([P, CH, KNOTS], BF16)
-            nc.sync.dma_start(out=graw[:], in_=grid.rearrange("(c p) m -> p c m", p=P))
+            nc.scalar.dma_start(out=graw[:], in_=grid.rearrange("(c p) m -> p c m", p=P))
+            xs = st.tile([P, BT, IN], BF16)
+            x_v = x.rearrange("(t p) i -> p t i", p=P)
+            for c2 in range(CH // 2):
+                nc.sync.dma_start(out=xs[:, :, c2 * 256 : (c2 + 1) * 256], in_=x_v[:, :, c2 * 256 : (c2 + 1) * 256])
 
             nc.vector.tensor_copy(out=knot[:], in_=graw[:])
             nc.vector.tensor_scalar(out=nknot[:], in0=knot[:], scalar1=-1.0, scalar2=None, op0=ALU.mult)
@@ -100,7 +183,12 @@ def tile_bsplinekanlayer_kernel(
                         nc.tensor.transpose(
                             ptx[:, cc, t * P : (t + 1) * P], xs[:, t, c * P : (c + 1) * P], ident_bf[:]
                         )
-                nc.vector.tensor_copy(out=xT[:, 2 * c2 : 2 * c2 + 2, :], in_=ptx[:])
+                if c2 == 0:
+                    nc.vector.tensor_copy(out=xT[:, 0:2, :], in_=ptx[:])
+                    for s in range(FIRST):
+                        bs_step(0, s)
+                else:
+                    nc.vector.tensor_copy(out=xT[:, 2 * c2 : 2 * c2 + 2, :], in_=ptx[:])
 
             sg = st.tile([P, 2, 4 * B], BF16, align_bytes=64)
             for g in range(2):
@@ -125,59 +213,7 @@ def tile_bsplinekanlayer_kernel(
                 in_=sg[:].rearrange("p g n -> p (g n)"),
             )
 
-        wk = ctx.enter_context(tc.tile_pool(name="work", bufs=3))
-        live = {}
-
-        def bs_step(c, m):
-            v = xT[:, c, :]
-            sq = wk.tile([P, B], F32, name="sq")
-            nc.scalar.activation(out=sq[:], in_=v, func=ACT.Square, bias=nknot[:, c, m : m + 1], scale=1.0)
-            z = wk.tile([P, B], F32, name="z")
-            nc.vector.scalar_tensor_tensor(
-                out=z[:], in0=v, scalar=knot[:, c, m : m + 1], in1=sq[:], op0=ALU.subtract, op1=ALU.mult
-            )
-            if m <= 8:
-                ra = wk.tile([P, B], F32, bufs=4, name="ra")
-                nc.scalar.activation(out=ra[:], in_=z[:], func=ACT.Relu, scale=ca[:, c, m : m + 1])
-                live[("ra", m)] = ra
-            if m >= 3:
-                la = wk.tile([P, B], F32, bufs=4, name="la")
-                nc.scalar.activation(out=la[:], in_=z[:], func=ACT.Relu, scale=ce[:, c, m - 3 : m - 2])
-                live[("la", m)] = la
-            if 1 <= m <= 8:
-                j = m - 1
-                if j % 4 == 0:
-                    live[("apl", j // 4)] = wk.tile([P, 4, B], BF16, name="apl")
-                nc.vector.scalar_tensor_tensor(
-                    out=live[("apl", j // 4)][:, j % 4, :], in0=live[("ra", m)][:], scalar=nbeta[:, c, j : j + 1],
-                    in1=live[("ra", m - 1)][:], op0=ALU.mult, op1=ALU.add,
-                )
-            if m >= 4:
-                j = m - 4
-                if j % 4 == 0:
-                    live[("bpl", j // 4)] = wk.tile([P, 4, B], BF16, name="bpl")
-                nc.vector.scalar_tensor_tensor(
-                    out=live[("bpl", j // 4)][:, j % 4, :], in0=live[("la", m - 1)][:], scalar=nphi[:, c, j : j + 1],
-                    in1=live[("la", m)][:], op0=ALU.mult, op1=ALU.add,
-                )
-                if j % 4 == 3:
-                    bs_finish(c, j // 4)
-
-        def bs_finish(c, h):
-            apl = live[("apl", h)]
-            nc.vector.tensor_tensor(out=apl[:], in0=apl[:], in1=live[("bpl", h)][:], op=ALU.max)
-            grp = wk.tile([P, B, 4], BF16, align_bytes=64, name="grp")
-            dst = grp[:].rearrange("p (c i) t -> p c t i", i=4)
-            src = apl[:].rearrange("p t (c i) -> p c t i", i=4)
-            if (c, h) in V_REGROUP:
-                nc.vector.tensor_copy(out=dst, in_=src)
-            else:
-                nc.scalar.copy(out=dst, in_=src)
-            nc.vector.quantize_mx(
-                out=bsc[c][:, h, :].bitcast(FP8X4), scales=bss[c][:, h, :], in_=grp[:].rearrange("p b t -> p (b t)")
-            )
-
-        with tc.tile_pool(name="swp", bufs=3) as swp, tc.tile_pool(name="sws", bufs=3) as sws, tc.psum_pool(
+        with tc.tile_pool(name="swp", bufs=2) as swp, tc.tile_pool(name="sws", bufs=3) as sws, tc.psum_pool(
             name="pswt", bufs=4
         ) as pswt, tc.psum_pool(name="psc", bufs=2) as psc:
             for g in range(2):
@@ -189,58 +225,56 @@ def tile_bsplinekanlayer_kernel(
             for g in range(2):
                 nc.sync.dma_start(out=wq[:, g, :].bitcast(I32), in_=base_weight_words[g].bitcast(I32))
 
-            def ssw_unit(ot, c):
-                rows = slice(ot * P, (ot + 1) * P)
-                if c == 0:
-                    sct = sws.tile([P, IN], BF16, bufs=2, name="sct")
-                    nc.sync.dma_start(out=sct[:], in_=spline_scaler[rows, :])
+            def ssw_unit(op, c, h):
+                rows = slice(op * 2 * P, (op + 1) * 2 * P)
+                if c == 0 and h == 0:
+                    sct = sws.tile([P, 2, IN], BF16, bufs=2, name="sct")
+                    nc.sync.dma_start(out=sct[:], in_=spline_scaler[rows, :].rearrange("(a o) i -> o a i", o=P))
                     live["sct"] = sct
-                if c % 4 == 0:
-                    pq = psc.tile([P, 4, 2 * P], BF16, name="pq")
-                    for cl in range(4):
-                        nc.tensor.matmul(
-                            out=pq[:, cl, :], lhsT=live["sct"][:, (c + cl) * P : (c + cl + 1) * P],
-                            rhs=e2[:].rearrange("p o e -> p (o e)"), start=True, stop=True,
-                        )
-                    sc2 = sws.tile([P, 4, 2, 2 * P], BF16, name="sc2")
-                    nc.scalar.copy(out=sc2[:], in_=pq[:].unsqueeze(2).to_broadcast([P, 4, 2, 2 * P]))
+                if c % 2 == 0 and h == 0:
+                    pq = psc.tile([P, 2, 2, 2 * P], BF16, name="pq")
+                    for cl in range(2):
+                        for a in range(2):
+                            nc.tensor.matmul(
+                                out=pq[:, cl, a, :], lhsT=live["sct"][:, a, (c + cl) * P : (c + cl + 1) * P],
+                                rhs=e2[:].rearrange("p o e -> p (o e)"), start=True, stop=True,
+                            )
+                    sc2 = sws.tile([P, 2, 4 * P], BF16, name="sc2")
+                    nc.scalar.copy(out=sc2[:], in_=pq[:].rearrange("p c a n -> p c (a n)"))
                     live["sc2"] = sc2
-                if c % 2 == 0:
-                    swt = swp.tile([P, 2 * P * NB], BF16, name="swt")
+                    swt = swp.tile([P, 2, 2 * P * NB], BF16, name="swt")
                     nc.sync.dma_start(
                         out=swt[:],
-                        in_=spline_weight[rows, c * P : (c + 2) * P, :].rearrange("o i j -> o (i j)"),
+                        in_=spline_weight[rows, c * P : (c + 2) * P, :].rearrange("(a o) i j -> o a (i j)", o=P),
                     )
                     live["swt"] = swt
                 sww = live["swt"][:].bitcast(F32)
                 cl = c % 2
-                bank = pswt.tile([P, 4, P], F32, name="bank")
-                for jj in range(4):
-                    nc.tensor.transpose(
-                        bank[:, (jj % 2) * 2 + jj // 2, :], sww[:, 512 * cl + jj : 512 * (cl + 1) : 4], ident_f[:]
-                    )
+                bank = pswt.tile([P, 2, 2, P], F32, name="bank")
+                for a in range(2):
+                    for u in range(2):
+                        nc.tensor.transpose(
+                            bank[:, u, a, :], sww[:, a, 512 * cl + 2 * h + u : 512 * (cl + 1) : 4], ident_f[:]
+                        )
                 gt = sws.tile([P, 8 * P], BF16, align_bytes=64, name="gt")
                 nc.vector.tensor_tensor(
                     out=gt[:].rearrange("p (q u e) -> p q u e", u=2, e=2),
-                    in0=bank[:].rearrange("p a o -> p (a o)").bitcast(BF16).rearrange("p (u q e) -> p q u e", u=2, e=2),
-                    in1=live["sc2"][:, c % 4].rearrange("p h n -> p (h n)").rearrange("p (q e) -> p q e", e=2)
-                    .unsqueeze(2).to_broadcast([P, 2 * P, 2, 2]),
+                    in0=bank[:].rearrange("p u a o -> p (u a o)").bitcast(BF16).rearrange("p (u q e) -> p q u e", u=2, e=2),
+                    in1=live["sc2"][:, cl, :].rearrange("p (q e) -> p q e", e=2).unsqueeze(2).to_broadcast([P, 2 * P, 2, 2]),
                     op=ALU.mult,
                 )
-                for h in range(2):
-                    nc.vector.quantize_mx(
-                        out=sswc[:, 2 * c + h, rows].bitcast(FP8X4), scales=ssws[:, 2 * c + h, rows],
-                        in_=gt[:, h * 4 * P : (h + 1) * 4 * P],
-                    )
+                nc.vector.quantize_mx(
+                    out=sswc[:, 2 * c + h, rows].bitcast(FP8X4), scales=ssws[:, 2 * c + h, rows], in_=gt[:]
+                )
 
-            units = [(ot, c) for ot in range(OT) for c in range(CH)]
+            units = [(op, c, h) for op in range(OT // 2) for c in range(CH) for h in range(2)]
             steps = EARLY * KNOTS
             done = 0
-            for s in range(steps):
+            for s in range(FIRST, steps):
                 bs_step(s // KNOTS, s % KNOTS)
                 want = ((s + 1) * len(units) + steps - 1) // steps
                 while done < min(want, len(units)):
-                    ssw_unit(units[done][0], units[done][1])
+                    ssw_unit(units[done][0], units[done][1], units[done][2])
                     done += 1
 
         pacc = ctx.enter_context(tc.psum_pool(name="pacc", bufs=1))

@@ -63,6 +63,8 @@ def tile_bsplinekanlayer_kernel(
 
         wk = ctx.enter_context(tc.tile_pool(name="work", bufs=3))
         live = {}
+        later = []
+        live["lp"] = 0
 
         def st_sq(c, m):
             sq = wk.tile([P, B], F32, bufs=4, name="sq")
@@ -106,7 +108,8 @@ def tile_bsplinekanlayer_kernel(
                     in1=live[("la", c, m)][:], op0=ALU.mult, op1=ALU.add,
                 )
                 if j % 4 == 3:
-                    bs_finish(c, j // 4)
+                    s = c * KNOTS + m
+                    later.append((s + 1, fin_max, c, j // 4, live[("apl", j // 4)], live[("bpl", j // 4)]))
 
         def bs_step(c, m):
             s = c * KNOTS + m
@@ -124,10 +127,16 @@ def tile_bsplinekanlayer_kernel(
             if s + 1 < CH * KNOTS:
                 st_relu((s + 1) // KNOTS, (s + 1) % KNOTS)
             st_ab(c, m)
+            run_later(s)
 
-        def bs_finish(c, h):
-            apl = live[("apl", h)]
-            nc.vector.tensor_tensor(out=apl[:], in0=apl[:], in1=live[("bpl", h)][:], op=ALU.max)
+        def run_later(s, flush=False):
+            while live["lp"] < len(later) and (flush or later[live["lp"]][0] <= s):
+                item = later[live["lp"]]
+                live["lp"] += 1
+                item[1](s, item[2], item[3], item[4], item[5])
+
+        def fin_max(s, c, h, apl, bpl):
+            nc.vector.tensor_tensor(out=apl[:], in0=apl[:], in1=bpl[:], op=ALU.max)
             grp = wk.tile([P, B, 4], BF16, bufs=2, align_bytes=64, name="grp")
             dst = grp[:].rearrange("p (c i) t -> p c t i", i=4)
             src = apl[:].rearrange("p t (c i) -> p c t i", i=4)
@@ -135,6 +144,9 @@ def tile_bsplinekanlayer_kernel(
                 nc.vector.tensor_copy(out=dst, in_=src)
             else:
                 nc.scalar.copy(out=dst, in_=src)
+            later.append((s + 2, fin_quant, c, h, grp, None))
+
+        def fin_quant(s, c, h, grp, unused):
             nc.vector.quantize_mx(
                 out=bsc[c][:, h, :].bitcast(FP8X4), scales=bss[c][:, h, :], in_=grp[:].rearrange("p b t -> p (b t)")
             )
@@ -263,9 +275,14 @@ def tile_bsplinekanlayer_kernel(
                     in1=live["sc2"][:, cl, :].rearrange("p (q e) -> p q e", e=2).unsqueeze(2).to_broadcast([P, 2 * P, 2, 2]),
                     op=ALU.mult,
                 )
-                nc.vector.quantize_mx(
-                    out=sswc[:, 2 * c + h, rows].bitcast(FP8X4), scales=ssws[:, 2 * c + h, rows], in_=gt[:]
-                )
+                ssw_quant()
+                live["pend"] = (gt, 2 * c + h, rows)
+
+            def ssw_quant():
+                if live.get("pend") is not None:
+                    gt, ps, rows = live["pend"]
+                    nc.vector.quantize_mx(out=sswc[:, ps, rows].bitcast(FP8X4), scales=ssws[:, ps, rows], in_=gt[:])
+                    live["pend"] = None
 
             units = [(op, c, h) for op in range(OT // 2) for c in range(CH) for h in range(2)]
             steps = EARLY * KNOTS
@@ -276,6 +293,8 @@ def tile_bsplinekanlayer_kernel(
                 while done < min(want, len(units)):
                     ssw_unit(units[done][0], units[done][1], units[done][2])
                     done += 1
+            ssw_quant()
+            run_later(steps, flush=True)
 
         pacc = ctx.enter_context(tc.psum_pool(name="pacc", bufs=1))
         late = ctx.enter_context(tc.tile_pool(name="late", bufs=1))
@@ -314,9 +333,12 @@ def tile_bsplinekanlayer_kernel(
             bss[c] = late.tile([P, 2, B], U8, align_bytes=64, name="bss%d" % c)
             for m in range(KNOTS):
                 bs_step(c, m)
-                if m == 9:
+                if m == 3 and c > EARLY:
+                    mx_passes(c - 1, 1)
+                if m == 11:
                     mx_passes(c, 0)
-            mx_passes(c, 1)
+        run_later(CH * KNOTS, flush=True)
+        mx_passes(CH - 1, 1)
 
         n = 0
         for t in range(BT):

@@ -22,6 +22,7 @@ FLOPS = 2 * B * OUT * (IN * NB + IN)
 EARLY = 6
 V_REGROUP = ((7, 1),)
 FIRST = 8
+PE_A = (3, 4, 5, 6, 7)
 
 
 def tile_bsplinekanlayer_kernel(
@@ -37,15 +38,16 @@ def tile_bsplinekanlayer_kernel(
         make_identity(nc, ident_f[:])
         warm = const.tile([P, 1], F32)
         nc.scalar.activation(out=warm[:], in_=ident_f[:, 0:1], func=ACT.Silu)
-        e2 = const.tile([P, P, 2], BF16)
-        nc.vector.tensor_copy(out=e2[:], in_=ident_bf[:].unsqueeze(2).to_broadcast([P, P, 2]))
 
         knot = const.tile([P, CH, KNOTS], F32)
         nknot = const.tile([P, CH, KNOTS], F32)
         ca = const.tile([P, CH, 9], F32)
         ce = const.tile([P, CH, 9], F32)
-        nbeta = const.tile([P, CH, 8], F32)
-        nphi = const.tile([P, CH, 8], F32)
+        cb = const.tile([P, CH, 8], F32)
+        cf = const.tile([P, CH, 8], F32)
+        cbr = const.tile([P, CH, 8], F32)
+        nident_f = const.tile([P, P], F32)
+        nc.vector.tensor_scalar(out=nident_f[:], in0=ident_f[:], scalar1=-1.0, scalar2=None, op0=ALU.mult)
         xT = const.tile([P, CH, B], BF16)
         sxc = const.tile([P, 2, B], U32, align_bytes=64)
         sxs = const.tile([P, 2, B], U8, align_bytes=64)
@@ -66,13 +68,16 @@ def tile_bsplinekanlayer_kernel(
         later = []
         live["lp"] = 0
 
+        def on_pe(c, j):
+            return j in PE_A and FIRST <= c * KNOTS + j + 1 < EARLY * KNOTS
+
         def st_sq(c, m):
             sq = wk.tile([P, B], F32, bufs=4, name="sq")
             nc.scalar.activation(out=sq[:], in_=xT[:, c, :], func=ACT.Square, bias=nknot[:, c, m : m + 1], scale=1.0)
             live[("sq", c, m)] = sq
 
         def st_z(c, m):
-            z = wk.tile([P, B], F32, bufs=4, name="z")
+            z = wk.tile([P, B], F32, bufs=5, name="z")
             nc.vector.scalar_tensor_tensor(
                 out=z[:], in0=xT[:, c, :], scalar=knot[:, c, m : m + 1], in1=live[("sq", c, m)][:],
                 op0=ALU.subtract, op1=ALU.mult,
@@ -81,31 +86,40 @@ def tile_bsplinekanlayer_kernel(
 
         def st_relu(c, m):
             z = live[("z", c, m)]
-            if m <= 8:
-                ra = wk.tile([P, B], F32, bufs=5, name="ra")
-                nc.scalar.activation(out=ra[:], in_=z[:], func=ACT.Relu, scale=ca[:, c, m : m + 1])
-                live[("ra", c, m)] = ra
-            if m >= 3:
-                la = wk.tile([P, B], F32, bufs=5, name="la")
-                nc.scalar.activation(out=la[:], in_=z[:], func=ACT.Relu, scale=ce[:, c, m - 3 : m - 2])
-                live[("la", c, m)] = la
+            if 1 <= m <= 8:
+                rb = wk.tile([P, B], F32, bufs=4, name="rb")
+                coef = cbr if on_pe(c, m - 1) else cb
+                nc.scalar.activation(out=rb[:], in_=z[:], func=ACT.Relu, scale=coef[:, c, m - 1 : m])
+                live[("rb", c, m)] = rb
+            if 3 <= m <= 10:
+                lb = wk.tile([P, B], F32, bufs=4, name="lb")
+                nc.scalar.activation(out=lb[:], in_=z[:], func=ACT.Relu, scale=cf[:, c, m - 3 : m - 2])
+                live[("lb", c, m)] = lb
 
         def st_ab(c, m):
             if 1 <= m <= 8:
                 j = m - 1
                 if j % 4 == 0:
                     live[("apl", j // 4)] = wk.tile([P, 4, B], BF16, bufs=2, name="apl")
-                nc.vector.scalar_tensor_tensor(
-                    out=live[("apl", j // 4)][:, j % 4, :], in0=live[("ra", c, m)][:], scalar=nbeta[:, c, j : j + 1],
-                    in1=live[("ra", c, m - 1)][:], op0=ALU.mult, op1=ALU.add,
-                )
+                if on_pe(c, j):
+                    pd = live["psum"].tile([P, B], F32, name="pd")
+                    nc.tensor.matmul(out=pd[:], lhsT=ident_f[:], rhs=live[("z", c, m - 1)][:], start=True, stop=False)
+                    nc.tensor.matmul(out=pd[:], lhsT=nident_f[:], rhs=live[("rb", c, m)][:], start=False, stop=True)
+                    nc.scalar.activation(
+                        out=live[("apl", j // 4)][:, j % 4, :], in_=pd[:], func=ACT.Copy, scale=ca[:, c, j : j + 1]
+                    )
+                else:
+                    nc.vector.scalar_tensor_tensor(
+                        out=live[("apl", j // 4)][:, j % 4, :], in0=live[("z", c, m - 1)][:], scalar=ca[:, c, j : j + 1],
+                        in1=live[("rb", c, m)][:], op0=ALU.mult, op1=ALU.subtract,
+                    )
             if m >= 4:
                 j = m - 4
                 if j % 4 == 0:
                     live[("bpl", j // 4)] = wk.tile([P, 4, B], BF16, bufs=2, name="bpl")
                 nc.vector.scalar_tensor_tensor(
-                    out=live[("bpl", j // 4)][:, j % 4, :], in0=live[("la", c, m - 1)][:], scalar=nphi[:, c, j : j + 1],
-                    in1=live[("la", c, m)][:], op0=ALU.mult, op1=ALU.add,
+                    out=live[("bpl", j // 4)][:, j % 4, :], in0=live[("z", c, m)][:], scalar=ce[:, c, j + 1 : j + 2],
+                    in1=live[("lb", c, m - 1)][:], op0=ALU.mult, op1=ALU.subtract,
                 )
                 if j % 4 == 3:
                     s = c * KNOTS + m
@@ -141,9 +155,9 @@ def tile_bsplinekanlayer_kernel(
             dst = grp[:].rearrange("p (c i) t -> p c t i", i=4)
             src = apl[:].rearrange("p t (c i) -> p c t i", i=4)
             if (c, h) in V_REGROUP:
-                nc.vector.tensor_copy(out=dst, in_=src)
+                nc.vector.tensor_scalar(out=dst, in0=src, scalar1=0.0, scalar2=None, op0=ALU.max)
             else:
-                nc.scalar.copy(out=dst, in_=src)
+                nc.scalar.activation(out=dst, in_=src, func=ACT.Relu)
             later.append((s + 2, fin_quant, c, h, grp, None))
 
         def fin_quant(s, c, h, grp, unused):
@@ -180,12 +194,11 @@ def tile_bsplinekanlayer_kernel(
             nc.vector.reciprocal(out=pe[:], in_=pe[:])
             nc.vector.tensor_scalar(out=ce[:], in0=pe[:], scalar1=-1.0, scalar2=None, op0=ALU.mult)
             nc.vector.reciprocal(out=r1[:], in_=d1[:])
-            nc.vector.scalar_tensor_tensor(
-                out=nbeta[:], in0=d4[:], scalar=-1.0, in1=r1[:, :, 0:8], op0=ALU.mult, op1=ALU.mult
-            )
-            nc.vector.scalar_tensor_tensor(
-                out=nphi[:], in0=d4[:], scalar=-1.0, in1=r1[:, :, 3:11], op0=ALU.mult, op1=ALU.mult
-            )
+            nc.vector.tensor_tensor(out=cb[:], in0=d4[:], in1=r1[:, :, 0:8], op=ALU.mult)
+            nc.vector.tensor_tensor(out=cb[:], in0=cb[:], in1=ca[:, :, 1:9], op=ALU.mult)
+            nc.vector.tensor_tensor(out=cbr[:], in0=cb[:], in1=pa[:, :, 0:8], op=ALU.mult)
+            nc.vector.tensor_tensor(out=cf[:], in0=d4[:], in1=r1[:, :, 3:11], op=ALU.mult)
+            nc.vector.tensor_tensor(out=cf[:], in0=cf[:], in1=ce[:, :, 0:8], op=ALU.mult)
 
             for c2 in range(CH // 2):
                 ptx = ps0.tile([P, 2, B], BF16)
@@ -227,7 +240,8 @@ def tile_bsplinekanlayer_kernel(
 
         with tc.tile_pool(name="swp", bufs=2) as swp, tc.tile_pool(name="sws", bufs=3) as sws, tc.psum_pool(
             name="pswt", bufs=4
-        ) as pswt, tc.psum_pool(name="psc", bufs=2) as psc:
+        ) as pswt, tc.psum_pool(name="psc", bufs=2) as psc, tc.psum_pool(name="psd", bufs=2) as psd:
+            live["psum"] = psd
             for g in range(2):
                 for q in range(4):
                     nc.sync.dma_start(
@@ -244,15 +258,17 @@ def tile_bsplinekanlayer_kernel(
                     nc.sync.dma_start(out=sct[:], in_=spline_scaler[rows, :].rearrange("(a o) i -> o a i", o=P))
                     live["sct"] = sct
                 if c % 2 == 0 and h == 0:
-                    pq = psc.tile([P, 2, 2, 2 * P], BF16, name="pq")
+                    pq = psc.tile([P, 2, 2, P], BF16, name="pq")
                     for cl in range(2):
                         for a in range(2):
-                            nc.tensor.matmul(
-                                out=pq[:, cl, a, :], lhsT=live["sct"][:, a, (c + cl) * P : (c + cl + 1) * P],
-                                rhs=e2[:].rearrange("p o e -> p (o e)"), start=True, stop=True,
+                            nc.tensor.transpose(
+                                pq[:, cl, a, :], live["sct"][:, a, (c + cl) * P : (c + cl + 1) * P], ident_bf[:]
                             )
                     sc2 = sws.tile([P, 2, 4 * P], BF16, name="sc2")
-                    nc.scalar.copy(out=sc2[:], in_=pq[:].rearrange("p c a n -> p c (a n)"))
+                    nc.scalar.copy(
+                        out=sc2[:].rearrange("p c (q e) -> p c q e", e=2),
+                        in_=pq[:].rearrange("p c a o -> p c (a o)").unsqueeze(3).to_broadcast([P, 2, 2 * P, 2]),
+                    )
                     live["sc2"] = sc2
                     swt = swp.tile([P, 2, 2 * P * NB], BF16, name="swt")
                     nc.sync.dma_start(

@@ -20,7 +20,7 @@ BT = B // P
 OT = OUT // P
 FLOPS = 2 * B * OUT * (IN * NB + IN)
 EARLY = 6
-V_REGROUP = ((7, 1),)
+LAST = (7, 1)
 FIRST = 8
 PE_A = (3, 4, 5, 6, 7)
 
@@ -72,7 +72,7 @@ def tile_bsplinekanlayer_kernel(
             return j in PE_A and FIRST <= c * KNOTS + j + 1 < EARLY * KNOTS
 
         def st_sq(c, m):
-            sq = wk.tile([P, B], F32, bufs=4, name="sq")
+            sq = wk.tile([P, B], F32, bufs=5, name="sq")
             nc.scalar.activation(out=sq[:], in_=xT[:, c, :], func=ACT.Square, bias=nknot[:, c, m : m + 1], scale=1.0)
             live[("sq", c, m)] = sq
 
@@ -87,12 +87,12 @@ def tile_bsplinekanlayer_kernel(
         def st_relu(c, m):
             z = live[("z", c, m)]
             if 1 <= m <= 8:
-                rb = wk.tile([P, B], F32, bufs=4, name="rb")
+                rb = wk.tile([P, B], F32, bufs=6, name="rb")
                 coef = cbr if on_pe(c, m - 1) else cb
                 nc.scalar.activation(out=rb[:], in_=z[:], func=ACT.Relu, scale=coef[:, c, m - 1 : m])
                 live[("rb", c, m)] = rb
             if 3 <= m <= 10:
-                lb = wk.tile([P, B], F32, bufs=4, name="lb")
+                lb = wk.tile([P, B], F32, bufs=6, name="lb")
                 nc.scalar.activation(out=lb[:], in_=z[:], func=ACT.Relu, scale=cf[:, c, m - 3 : m - 2])
                 live[("lb", c, m)] = lb
 
@@ -150,15 +150,35 @@ def tile_bsplinekanlayer_kernel(
                 item[1](s, item[2], item[3], item[4], item[5])
 
         def fin_max(s, c, h, apl, bpl):
-            nc.vector.tensor_tensor(out=apl[:], in0=apl[:], in1=bpl[:], op=ALU.max)
             grp = wk.tile([P, B, 4], BF16, bufs=2, align_bytes=64, name="grp")
+            if (c, h) == LAST:
+                fin_last(c, h, apl, bpl, grp)
+                return
+            nc.vector.tensor_tensor(out=apl[:], in0=apl[:], in1=bpl[:], op=ALU.max)
             dst = grp[:].rearrange("p (c i) t -> p c t i", i=4)
             src = apl[:].rearrange("p t (c i) -> p c t i", i=4)
-            if (c, h) in V_REGROUP:
-                nc.vector.tensor_scalar(out=dst, in0=src, scalar1=0.0, scalar2=None, op0=ALU.max)
-            else:
-                nc.scalar.activation(out=dst, in_=src, func=ACT.Relu)
+            nc.scalar.activation(out=dst, in_=src, func=ACT.Relu)
             later.append((s + 2, fin_quant, c, h, grp, None))
+
+        def fin_last(c, h, apl, bpl, grp):
+            half = B // 2
+            for k in range(2):
+                cols = slice(k * half, (k + 1) * half)
+                nc.vector.tensor_tensor(out=apl[:, :, cols], in0=apl[:, :, cols], in1=bpl[:, :, cols], op=ALU.max)
+            for k in range(2):
+                cols = slice(k * half, (k + 1) * half)
+                dst = grp[:, cols, :].rearrange("p (c i) t -> p c t i", i=4)
+                src = apl[:, :, cols].rearrange("p t (c i) -> p c t i", i=4)
+                if k == 0:
+                    nc.vector.tensor_scalar(out=dst, in0=src, scalar1=0.0, scalar2=None, op0=ALU.max)
+                else:
+                    nc.scalar.activation(out=dst, in_=src, func=ACT.Relu)
+            for k in range(2):
+                cols = slice(k * half, (k + 1) * half)
+                nc.vector.quantize_mx(
+                    out=bsc[c][:, h, cols].bitcast(FP8X4), scales=bss[c][:, h, cols],
+                    in_=grp[:, cols, :].rearrange("p b t -> p (b t)"),
+                )
 
         def fin_quant(s, c, h, grp, unused):
             nc.vector.quantize_mx(

from contextlib import ExitStack

import concourse.mybir as mybir
from concourse.masks import make_identity

F32 = mybir.dt.float32
BF16 = mybir.dt.bfloat16
U8 = mybir.dt.uint8
U32 = mybir.dt.uint32
I32 = mybir.dt.int32
FP8X4 = mybir.dt.float8_e4m3fn_x4
FP4X4 = mybir.dt.float4_e2m1fn_x4
ALU = mybir.AluOpType
ACT = mybir.ActivationFunctionType

P = 128
B, IN, OUT, NB, KNOTS = 512, 1024, 1024, 8, 12
CH = IN // P
BT = B // P
OT = OUT // P
FLOPS = 2 * B * OUT * (IN * NB + IN)
EARLY = 6
LAST = (7, 1)
FIRST = 8
PE_A = (3, 4, 5, 6, 7)


def tile_bsplinekanlayer_kernel(
    tc, x, base_weight_words, base_weight_scales, spline_weight, spline_scaler, grid, out
):
    nc = tc.nc
    with ExitStack() as ctx:
        const = ctx.enter_context(tc.tile_pool(name="const", bufs=1))

        ident_bf = const.tile([P, P], BF16)
        make_identity(nc, ident_bf[:])
        ident_f = const.tile([P, P], F32)
        make_identity(nc, ident_f[:])
        warm = const.tile([P, 1], F32)
        nc.scalar.activation(out=warm[:], in_=ident_f[:, 0:1], func=ACT.Silu)

        knot = const.tile([P, CH, KNOTS], F32)
        nknot = const.tile([P, CH, KNOTS], F32)
        ca = const.tile([P, CH, 9], F32)
        ce = const.tile([P, CH, 9], F32)
        cb = const.tile([P, CH, 8], F32)
        cf = const.tile([P, CH, 8], F32)
        cbr = const.tile([P, CH, 8], F32)
        nident_f = const.tile([P, P], F32)
        nc.vector.tensor_scalar(out=nident_f[:], in0=ident_f[:], scalar1=-1.0, scalar2=None, op0=ALU.mult)
        xT = const.tile([P, CH, B], BF16)
        sxc = const.tile([P, 2, B], U32, align_bytes=64)
        sxs = const.tile([P, 2, B], U8, align_bytes=64)
        wq = const.tile([P, 2, 2 * OUT], U8, align_bytes=64)
        wsc = const.tile([P, 2, OUT], U8, align_bytes=64)
        sswc = const.tile([P, 2 * CH, OUT], U32, align_bytes=64)
        ssws = const.tile([P, 2 * CH, OUT], U8, align_bytes=64)
        bsc = {}
        bss = {}
        for c in range(EARLY):
            bsc[c] = const.tile([P, 2, B], U32, align_bytes=64, name="bsc%d" % c)
            bss[c] = const.tile([P, 2, B], U8, align_bytes=64, name="bss%d" % c)

        nc.vector.memset(wsc[:].rearrange("p g n -> p (g n)").bitcast(I32), 0)

        wk = ctx.enter_context(tc.tile_pool(name="work", bufs=3))
        live = {}
        later = []
        live["lp"] = 0

        def on_pe(c, j):
            return j in PE_A and FIRST <= c * KNOTS + j + 1 < EARLY * KNOTS

        def st_sq(c, m):
            sq = wk.tile([P, B], F32, bufs=5, name="sq")
            nc.scalar.activation(out=sq[:], in_=xT[:, c, :], func=ACT.Square, bias=nknot[:, c, m : m + 1], scale=1.0)
            live[("sq", c, m)] = sq

        def st_z(c, m):
            z = wk.tile([P, B], F32, bufs=5, name="z")
            nc.vector.scalar_tensor_tensor(
                out=z[:], in0=xT[:, c, :], scalar=knot[:, c, m : m + 1], in1=live[("sq", c, m)][:],
                op0=ALU.subtract, op1=ALU.mult,
            )
            live[("z", c, m)] = z

        def st_relu(c, m):
            z = live[("z", c, m)]
            if 1 <= m <= 8:
                rb = wk.tile([P, B], F32, bufs=6, name="rb")
                coef = cbr if on_pe(c, m - 1) else cb
                nc.scalar.activation(out=rb[:], in_=z[:], func=ACT.Relu, scale=coef[:, c, m - 1 : m])
                live[("rb", c, m)] = rb
            if 3 <= m <= 10:
                lb = wk.tile([P, B], F32, bufs=6, name="lb")
                nc.scalar.activation(out=lb[:], in_=z[:], func=ACT.Relu, scale=cf[:, c, m - 3 : m - 2])
                live[("lb", c, m)] = lb

        def st_ab(c, m):
            if 1 <= m <= 8:
                j = m - 1
                if j % 4 == 0:
                    live[("apl", j // 4)] = wk.tile([P, 4, B], BF16, bufs=2, name="apl")
                if on_pe(c, j):
                    pd = live["psum"].tile([P, B], F32, name="pd")
                    nc.tensor.matmul(out=pd[:], lhsT=ident_f[:], rhs=live[("z", c, m - 1)][:], start=True, stop=False)
                    nc.tensor.matmul(out=pd[:], lhsT=nident_f[:], rhs=live[("rb", c, m)][:], start=False, stop=True)
                    nc.scalar.activation(
                        out=live[("apl", j // 4)][:, j % 4, :], in_=pd[:], func=ACT.Copy, scale=ca[:, c, j : j + 1]
                    )
                else:
                    nc.vector.scalar_tensor_tensor(
                        out=live[("apl", j // 4)][:, j % 4, :], in0=live[("z", c, m - 1)][:], scalar=ca[:, c, j : j + 1],
                        in1=live[("rb", c, m)][:], op0=ALU.mult, op1=ALU.subtract,
                    )
            if m >= 4:
                j = m - 4
                if j % 4 == 0:
                    live[("bpl", j // 4)] = wk.tile([P, 4, B], BF16, bufs=2, name="bpl")
                nc.vector.scalar_tensor_tensor(
                    out=live[("bpl", j // 4)][:, j % 4, :], in0=live[("z", c, m)][:], scalar=ce[:, c, j + 1 : j + 2],
                    in1=live[("lb", c, m - 1)][:], op0=ALU.mult, op1=ALU.subtract,
                )
                if j % 4 == 3:
                    s = c * KNOTS + m
                    later.append((s + 1, fin_max, c, j // 4, live[("apl", j // 4)], live[("bpl", j // 4)]))

        def bs_step(c, m):
            s = c * KNOTS + m
            if s == 0:
                st_sq(0, 0)
                st_sq(0, 1)
                st_sq(0, 2)
                st_z(0, 0)
                st_z(0, 1)
                st_relu(0, 0)
            if s + 3 < CH * KNOTS:
                st_sq((s + 3) // KNOTS, (s + 3) % KNOTS)
            if s + 2 < CH * KNOTS:
                st_z((s + 2) // KNOTS, (s + 2) % KNOTS)
            if s + 1 < CH * KNOTS:
                st_relu((s + 1) // KNOTS, (s + 1) % KNOTS)
            st_ab(c, m)
            run_later(s)

        def run_later(s, flush=False):
            while live["lp"] < len(later) and (flush or later[live["lp"]][0] <= s):
                item = later[live["lp"]]
                live["lp"] += 1
                item[1](s, item[2], item[3], item[4], item[5])

        def fin_max(s, c, h, apl, bpl):
            grp = wk.tile([P, B, 4], BF16, bufs=2, align_bytes=64, name="grp")
            if (c, h) == LAST:
                fin_last(c, h, apl, bpl, grp)
                return
            nc.vector.tensor_tensor(out=apl[:], in0=apl[:], in1=bpl[:], op=ALU.max)
            dst = grp[:].rearrange("p (c i) t -> p c t i", i=4)
            src = apl[:].rearrange("p t (c i) -> p c t i", i=4)
            nc.scalar.activation(out=dst, in_=src, func=ACT.Relu)
            later.append((s + 2, fin_quant, c, h, grp, None))

        def fin_last(c, h, apl, bpl, grp):
            half = B // 2
            for k in range(2):
                cols = slice(k * half, (k + 1) * half)
                nc.vector.tensor_tensor(out=apl[:, :, cols], in0=apl[:, :, cols], in1=bpl[:, :, cols], op=ALU.max)
            for k in range(2):
                cols = slice(k * half, (k + 1) * half)
                dst = grp[:, cols, :].rearrange("p (c i) t -> p c t i", i=4)
                src = apl[:, :, cols].rearrange("p t (c i) -> p c t i", i=4)
                if k == 0:
                    nc.vector.tensor_scalar(out=dst, in0=src, scalar1=0.0, scalar2=None, op0=ALU.max)
                else:
                    nc.scalar.activation(out=dst, in_=src, func=ACT.Relu)
            for k in range(2):
                cols = slice(k * half, (k + 1) * half)
                nc.vector.quantize_mx(
                    out=bsc[c][:, h, cols].bitcast(FP8X4), scales=bss[c][:, h, cols],
                    in_=grp[:, cols, :].rearrange("p b t -> p (b t)"),
                )

        def fin_quant(s, c, h, grp, unused):
            nc.vector.quantize_mx(
                out=bsc[c][:, h, :].bitcast(FP8X4), scales=bss[c][:, h, :], in_=grp[:].rearrange("p b t -> p (b t)")
            )

        with tc.tile_pool(name="start", bufs=1) as st, tc.psum_pool(name="pstart", bufs=2) as ps0:
            graw = st.tile([P, CH, KNOTS], BF16)
            nc.scalar.dma_start(out=graw[:], in_=grid.rearrange("(c p) m -> p c m", p=P))
            xs = st.tile([P, BT, IN], BF16)
            x_v = x.rearrange("(t p) i -> p t i", p=P)
            for c2 in range(CH // 2):
                nc.sync.dma_start(out=xs[:, :, c2 * 256 : (c2 + 1) * 256], in_=x_v[:, :, c2 * 256 : (c2 + 1) * 256])

            nc.vector.tensor_copy(out=knot[:], in_=graw[:])
            nc.vector.tensor_scalar(out=nknot[:], in0=knot[:], scalar1=-1.0, scalar2=None, op0=ALU.mult)
            d1 = st.tile([P, CH, 11], F32)
            d2 = st.tile([P, CH, 10], F32)
            d3 = st.tile([P, CH, 9], F32)
            d4 = st.tile([P, CH, 8], F32)
            r1 = st.tile([P, CH, 11], F32)
            pa = st.tile([P, CH, 9], F32)
            pe = st.tile([P, CH, 9], F32)
            nc.vector.tensor_tensor(out=d1[:], in0=knot[:, :, 1:12], in1=knot[:, :, 0:11], op=ALU.subtract)
            nc.vector.tensor_tensor(out=d2[:], in0=knot[:, :, 2:12], in1=knot[:, :, 0:10], op=ALU.subtract)
            nc.vector.tensor_tensor(out=d3[:], in0=knot[:, :, 3:12], in1=knot[:, :, 0:9], op=ALU.subtract)
            nc.vector.tensor_tensor(out=d4[:], in0=knot[:, :, 4:12], in1=knot[:, :, 0:8], op=ALU.subtract)
            nc.vector.tensor_tensor(out=pa[:], in0=d1[:, :, 0:9], in1=d2[:, :, 0:9], op=ALU.mult)
            nc.vector.tensor_tensor(out=pa[:], in0=pa[:], in1=d3[:], op=ALU.mult)
            nc.vector.reciprocal(out=ca[:], in_=pa[:])
            nc.vector.tensor_tensor(out=pe[:], in0=d1[:, :, 2:11], in1=d2[:, :, 1:10], op=ALU.mult)
            nc.vector.tensor_tensor(out=pe[:], in0=pe[:], in1=d3[:], op=ALU.mult)
            nc.vector.reciprocal(out=pe[:], in_=pe[:])
            nc.vector.tensor_scalar(out=ce[:], in0=pe[:], scalar1=-1.0, scalar2=None, op0=ALU.mult)
            nc.vector.reciprocal(out=r1[:], in_=d1[:])
            nc.vector.tensor_tensor(out=cb[:], in0=d4[:], in1=r1[:, :, 0:8], op=ALU.mult)
            nc.vector.tensor_tensor(out=cb[:], in0=cb[:], in1=ca[:, :, 1:9], op=ALU.mult)
            nc.vector.tensor_tensor(out=cbr[:], in0=cb[:], in1=pa[:, :, 0:8], op=ALU.mult)
            nc.vector.tensor_tensor(out=cf[:], in0=d4[:], in1=r1[:, :, 3:11], op=ALU.mult)
            nc.vector.tensor_tensor(out=cf[:], in0=cf[:], in1=ce[:, :, 0:8], op=ALU.mult)

            for c2 in range(CH // 2):
                ptx = ps0.tile([P, 2, B], BF16)
                for cc in range(2):
                    c = 2 * c2 + cc
                    for t in range(BT):
                        nc.tensor.transpose(
                            ptx[:, cc, t * P : (t + 1) * P], xs[:, t, c * P : (c + 1) * P], ident_bf[:]
                        )
                if c2 == 0:
                    nc.vector.tensor_copy(out=xT[:, 0:2, :], in_=ptx[:])
                    for s in range(FIRST):
                        bs_step(0, s)
                else:
                    nc.vector.tensor_copy(out=xT[:, 2 * c2 : 2 * c2 + 2, :], in_=ptx[:])

            sg = st.tile([P, 2, 4 * B], BF16, align_bytes=64)
            for g in range(2):
                for hb in range(2):
                    pw = ps0.tile([P, 2, 2 * P], F32)
                    for u in range(2):
                        for t2 in range(2):
                            t = 2 * hb + t2
                            nc.tensor.transpose(
                                pw[:, u, t2 * P : (t2 + 1) * P],
                                xs[:, t, :].bitcast(F32)[:, 256 * g + u : 256 * (g + 1) : 2],
                                ident_f[:],
                            )
                    nc.scalar.activation(
                        out=sg[:, g, hb * 1024 : (hb + 1) * 1024].rearrange("p (b u e) -> p b u e", u=2, e=2),
                        in_=pw[:].bitcast(BF16).rearrange("p u (b e) -> p b u e", e=2),
                        func=ACT.Silu,
                    )
            nc.vector.quantize_mx(
                out=sxc[:].rearrange("p g n -> p (g n)").bitcast(FP8X4),
                scales=sxs[:].rearrange("p g n -> p (g n)"),
                in_=sg[:].rearrange("p g n -> p (g n)"),
            )

        with tc.tile_pool(name="swp", bufs=2) as swp, tc.tile_pool(name="sws", bufs=3) as sws, tc.psum_pool(
            name="pswt", bufs=4
        ) as pswt, tc.psum_pool(name="psc", bufs=2) as psc, tc.psum_pool(name="psd", bufs=2) as psd:
            live["psum"] = psd
            for g in range(2):
                for q in range(4):
                    nc.sync.dma_start(
                        out=wsc[32 * q : 32 * q + 4, g, :].bitcast(I32),
                        in_=base_weight_scales[g, 4 * q : 4 * q + 4, :].bitcast(I32),
                    )
            for g in range(2):
                nc.sync.dma_start(out=wq[:, g, :].bitcast(I32), in_=base_weight_words[g].bitcast(I32))

            def ssw_unit(op, c, h):
                rows = slice(op * 2 * P, (op + 1) * 2 * P)
                if c == 0 and h == 0:
                    sct = sws.tile([P, 2, IN], BF16, bufs=2, name="sct")
                    nc.sync.dma_start(out=sct[:], in_=spline_scaler[rows, :].rearrange("(a o) i -> o a i", o=P))
                    live["sct"] = sct
                if c % 2 == 0 and h == 0:
                    pq = psc.tile([P, 2, 2, P], BF16, name="pq")
                    for cl in range(2):
                        for a in range(2):
                            nc.tensor.transpose(
                                pq[:, cl, a, :], live["sct"][:, a, (c + cl) * P : (c + cl + 1) * P], ident_bf[:]
                            )
                    sc2 = sws.tile([P, 2, 4 * P], BF16, name="sc2")
                    nc.scalar.copy(
                        out=sc2[:].rearrange("p c (q e) -> p c q e", e=2),
                        in_=pq[:].rearrange("p c a o -> p c (a o)").unsqueeze(3).to_broadcast([P, 2, 2 * P, 2]),
                    )
                    live["sc2"] = sc2
                    swt = swp.tile([P, 2, 2 * P * NB], BF16, name="swt")
                    nc.sync.dma_start(
                        out=swt[:],
                        in_=spline_weight[rows, c * P : (c + 2) * P, :].rearrange("(a o) i j -> o a (i j)", o=P),
                    )
                    live["swt"] = swt
                sww = live["swt"][:].bitcast(F32)
                cl = c % 2
                bank = pswt.tile([P, 2, 2, P], F32, name="bank")
                for a in range(2):
                    for u in range(2):
                        nc.tensor.transpose(
                            bank[:, u, a, :], sww[:, a, 512 * cl + 2 * h + u : 512 * (cl + 1) : 4], ident_f[:]
                        )
                gt = sws.tile([P, 8 * P], BF16, align_bytes=64, name="gt")
                nc.vector.tensor_tensor(
                    out=gt[:].rearrange("p (q u e) -> p q u e", u=2, e=2),
                    in0=bank[:].rearrange("p u a o -> p (u a o)").bitcast(BF16).rearrange("p (u q e) -> p q u e", u=2, e=2),
                    in1=live["sc2"][:, cl, :].rearrange("p (q e) -> p q e", e=2).unsqueeze(2).to_broadcast([P, 2 * P, 2, 2]),
                    op=ALU.mult,
                )
                ssw_quant()
                live["pend"] = (gt, 2 * c + h, rows)

            def ssw_quant():
                if live.get("pend") is not None:
                    gt, ps, rows = live["pend"]
                    nc.vector.quantize_mx(out=sswc[:, ps, rows].bitcast(FP8X4), scales=ssws[:, ps, rows], in_=gt[:])
                    live["pend"] = None

            units = [(op, c, h) for op in range(OT // 2) for c in range(CH) for h in range(2)]
            steps = EARLY * KNOTS
            done = 0
            for s in range(FIRST, steps):
                bs_step(s // KNOTS, s % KNOTS)
                want = ((s + 1) * len(units) + steps - 1) // steps
                while done < min(want, len(units)):
                    ssw_unit(units[done][0], units[done][1], units[done][2])
                    done += 1
            ssw_quant()
            run_later(steps, flush=True)

        pacc = ctx.enter_context(tc.psum_pool(name="pacc", bufs=1))
        late = ctx.enter_context(tc.tile_pool(name="late", bufs=1))
        acc = {}
        for t in range(BT):
            for oh in range(2):
                acc[(t, oh)] = pacc.tile([P, 512], F32, name="acc%d%d" % (t, oh))
        for g in range(2):
            for t in range(BT):
                for oh in range(2):
                    nc.tensor.matmul_mx(
                        out=acc[(t, oh)][:],
                        lhsT=sxc[:, g, t * P : (t + 1) * P].bitcast(FP8X4), lhsT_scale=sxs[:, g, t * P : (t + 1) * P],
                        rhs=wq[:, g, oh * 1024 : (oh + 1) * 1024].bitcast(FP4X4),
                        rhs_scale=wsc[:, g, oh * 512 : (oh + 1) * 512],
                        start=(g == 0), stop=False,
                    )

        def mx_passes(c, h):
            for t in range(BT):
                for oh in range(2):
                    nc.tensor.matmul_mx(
                        out=acc[(t, oh)][:],
                        lhsT=bsc[c][:, h, t * P : (t + 1) * P].bitcast(FP8X4),
                        lhsT_scale=bss[c][:, h, t * P : (t + 1) * P],
                        rhs=sswc[:, 2 * c + h, oh * 512 : (oh + 1) * 512].bitcast(FP8X4),
                        rhs_scale=ssws[:, 2 * c + h, oh * 512 : (oh + 1) * 512],
                        start=False, stop=(c == CH - 1 and h == 1),
                    )

        for c in range(EARLY):
            mx_passes(c, 0)
            mx_passes(c, 1)
        for c in range(EARLY, CH):
            bsc[c] = late.tile([P, 2, B], U32, align_bytes=64, name="bsc%d" % c)
            bss[c] = late.tile([P, 2, B], U8, align_bytes=64, name="bss%d" % c)
            for m in range(KNOTS):
                bs_step(c, m)
                if m == 3 and c > EARLY:
                    mx_passes(c - 1, 1)
                if m == 11:
                    mx_passes(c, 0)
        run_later(CH * KNOTS, flush=True)
        mx_passes(CH - 1, 1)

        n = 0
        for t in range(BT):
            for oh in range(2):
                res = late.tile([P, 512], F32, bufs=4, name="res")
                if n % 2 == 0:
                    nc.scalar.copy(out=res[:], in_=acc[(t, oh)][:])
                else:
                    nc.vector.tensor_copy(out=res[:], in_=acc[(t, oh)][:])
                nc.sync.dma_start(out=out[t * P : (t + 1) * P, oh * 512 : (oh + 1) * 512], in_=res[:])
                n += 1
